import numpy as np
import ml_dtypes


def mxq(x, axis, fmt="e4m3"):
    dtype, down = {"e4m3": (ml_dtypes.float8_e4m3fn, 7), "e5m2": (ml_dtypes.float8_e5m2, 14)}[fmt]
    v = np.moveaxis(np.asarray(x, np.float32).astype(ml_dtypes.bfloat16).astype(np.float64), axis, -1)
    blocks = v.reshape(v.shape[:-1] + (-1, 32))
    amax = np.abs(blocks).max(-1, keepdims=True)
    byte = np.maximum(np.where(amax > 0, np.frexp(amax)[1] - 1 + 127, 0) - down, 1)
    scale = np.exp2(byte - 127.0)
    codes = (blocks / scale).astype(np.float32).astype(dtype).astype(np.float64)
    return np.moveaxis((codes * scale).reshape(v.shape), -1, axis)


WIDE = False


def mx_kscale(k):
    if not WIDE:
        return np.ones(k)
    levels = np.array([10, -10, 5, -5, 0])
    a = np.random.permutation(np.resize(levels, k // 512 * 4)).reshape(k // 512, 4)
    idx = np.arange(k)
    return np.exp2(a[idx // 512, idx % 128 // 32])


BF16 = ml_dtypes.bfloat16


def bf(x):
    return np.asarray(x, np.float32).astype(BF16)


def f64(x):
    return np.asarray(x).astype(np.float64)


B, S, D, F1, F2, F3, F4 = 128, 4, 256, 1024, 2048, 1024, 512
K = D + D


def setup_inputs():
    s, t = mx_kscale(K), mx_kscale(F1)
    return {"x1": bf(np.random.standard_normal((B, S, D)) * s[:D]),
            "x2": bf(np.random.standard_normal((B, S, D)) * s[D:]),
            "W1": bf(np.random.standard_normal((S, K, F1)) * 1.0 / np.sqrt(K) / s[None, :, None] * t[None, None, :]),
            "b1": bf(np.random.standard_normal((S, F1)) * 0.3 * t),
            "W2": bf(np.random.standard_normal((S, F1, F2)) * 1.4 / np.sqrt(F1) / t[None, :, None]),
            "b2": bf(np.random.standard_normal((S, F2)) * 0.3)}


def reference(x1, x2, W1, b1, W2, b2):
    x = np.concatenate([f64(x1), f64(x2)], axis=-1).transpose(1, 0, 2)
    h = np.maximum((mxq(x, 2, "e4m3") @ mxq(f64(W1), 1, "e4m3")) + f64(b1)[:, None, :], 0.0)
    y = (mxq(h, 2, "e4m3") @ mxq(f64(W2), 1, "e4m3")) + f64(b2)[:, None, :]
    return y.transpose(1, 0, 2)

@@ -1,0 +1,201 @@
+from contextlib import ExitStack
+
+import concourse.mybir as mybir
+from concourse.masks import make_identity
+
+BF16 = mybir.dt.bfloat16
+F32 = mybir.dt.float32
+U32 = mybir.dt.uint32
+U8 = mybir.dt.uint8
+FP8X4 = mybir.dt.float8_e4m3fn_x4
+RELU = mybir.ActivationFunctionType.Relu
+ADD = mybir.AluOpType.add
+
+P = 128
+PACK = 4
+K_PASS = P * PACK
+
+B, S, D, F1, F2 = 128, 4, 256, 1024, 2048
+K1 = 2 * D
+PASSES2 = F1 // K_PASS
+N_PASS = 512
+BLOCKS2 = F2 // N_PASS
+SPREAD = 1024
+RUN = 4
+
+FLOPS = 2 * B * S * (K1 * F1 + F1 * F2)
+
+
+def tile_simplefusionmodule_pa_kernel(tc, x1, x2, W1, b1, W2, b2, out):
+    nc = tc.nc
+    with ExitStack() as ctx:
+        const = ctx.enter_context(tc.tile_pool(name="const", bufs=1))
+        w1_pool = ctx.enter_context(tc.tile_pool(name="w1_pool", bufs=3))
+        w2_pool = ctx.enter_context(tc.tile_pool(name="w2_pool", bufs=3 * PASSES2))
+        grouped_pool = ctx.enter_context(tc.tile_pool(name="grouped_pool", bufs=6))
+        codes_pool = ctx.enter_context(tc.tile_pool(name="codes_pool", bufs=6))
+        style_pool = ctx.enter_context(tc.tile_pool(name="style_pool", bufs=2))
+        out_pool = ctx.enter_context(tc.tile_pool(name="out_pool", bufs=S * BLOCKS2))
+        prep_psum = ctx.enter_context(tc.psum_pool(name="prep_psum", bufs=2))
+        h_psum = ctx.enter_context(tc.psum_pool(name="h_psum", bufs=2))
+        acc_psum = ctx.enter_context(tc.psum_pool(name="acc_psum", bufs=BLOCKS2))
+
+        w1_raw = []
+        w2_raw = []
+
+        def load_w1(s):
+            w1 = w1_pool.tile([P, PACK, F1], BF16)
+            nc.sync.dma_start(out=w1[:], in_=W1[s].rearrange("(p t) f -> p t f", t=PACK))
+            w1_raw.append(w1)
+
+        def load_w2(s):
+            for g in range(PASSES2):
+                w2 = w2_pool.tile([P, PACK, F2], BF16)
+                rows = W2[s, g * K_PASS : (g + 1) * K_PASS, :]
+                nc.sync.dma_start(out=w2[:], in_=rows.rearrange("(t p) n -> p t n", p=P))
+                w2_raw.append(w2)
+
+        B1_ROWS = S * F1 // P
+        B2_ROWS = S * F2 // P
+        bias_rows = const.tile([P, P], BF16)
+        nc.sync.dma_start(
+            out=bias_rows[0:B1_ROWS, :], in_=b1.rearrange("s (c p) -> (s c) p", p=P)
+        )
+        nc.sync.dma_start(
+            out=bias_rows[B1_ROWS : B1_ROWS + B2_ROWS, :],
+            in_=b2.rearrange("s (c p) -> (s c) p", p=P),
+        )
+        nc.vector.memset(bias_rows[B1_ROWS + B2_ROWS : P, :], 0.0)
+
+        x_cat = const.tile([P, S, K1], BF16)
+        load_w1(0)
+        nc.sync.dma_start(out=x_cat[:, :, 0:D], in_=x1)
+        nc.sync.dma_start(out=x_cat[:, :, D:K1], in_=x2)
+        load_w2(0)
+        for s in range(1, 3):
+            load_w1(s)
+            load_w2(s)
+
+        ident_bf = const.tile([P, P], BF16)
+        make_identity(nc, ident_bf[:])
+        ident_f32 = const.tile([P, P], F32)
+        make_identity(nc, ident_f32[:])
+
+        bias_cols = prep_psum.tile([P, P], BF16, tag="prep")
+        nc.tensor.transpose(bias_cols[:], bias_rows[:], ident_bf[:])
+        b1_cols = const.tile([P, B1_ROWS], F32)
+        nc.vector.tensor_copy(out=b1_cols[:], in_=bias_cols[:, 0:B1_ROWS])
+        b2_cols = const.tile([P, B2_ROWS], BF16)
+        nc.vector.tensor_copy(out=b2_cols[:], in_=bias_cols[:, B1_ROWS : B1_ROWS + B2_ROWS])
+
+        x_words = x_cat[:].bitcast(F32)
+        x_grouped = const.tile([P, S, B, 2], F32, align_bytes=64)
+        for pair in range(S // 2):
+            x_t = prep_psum.tile([P, 2, 2, B], F32, tag="prep")
+            for i in range(2):
+                for u in range(2):
+                    nc.tensor.transpose(
+                        x_t[:, i, u, :], x_words[:, 2 * pair + i, u : K1 // 2 : 2], ident_f32[:]
+                    )
+            nc.vector.tensor_copy(
+                out=x_grouped[:, 2 * pair : 2 * pair + 2],
+                in_=x_t[:].rearrange("p s u b -> p s b u"),
+            )
+        x_codes = const.tile([P, S * B], U32, align_bytes=64)
+        x_scales = const.tile([P, S * B], U8, align_bytes=64)
+        nc.vector.quantize_mx(
+            out=x_codes[:].bitcast(FP8X4),
+            scales=x_scales[:],
+            in_=x_grouped[:].bitcast(BF16).rearrange("p s b t -> p (s b t)"),
+        )
+
+        def quantise_block(raw, block):
+            grouped = grouped_pool.tile([P, N_PASS, PACK], BF16, align_bytes=64)
+            copy = nc.vector.tensor_copy if block % 2 == 0 else nc.scalar.copy
+            copy(
+                out=grouped[:].rearrange("p (c i) t -> p c t i", i=RUN),
+                in_=raw.rearrange("p t (c i) -> p c t i", i=RUN),
+            )
+            codes = codes_pool.tile([P, N_PASS], U32, align_bytes=64)
+            scales = codes_pool.tile([P, N_PASS], U8, align_bytes=64)
+            nc.vector.quantize_mx(
+                out=codes[:].bitcast(FP8X4),
+                scales=scales[:],
+                in_=grouped[:].rearrange("p c t -> p (c t)"),
+            )
+            return codes, scales
+
+        for s in range(S):
+            b2_all = style_pool.tile([P, F2], BF16)
+            for w in range(F2 // SPREAD):
+                spread = prep_psum.tile([P, SPREAD], BF16, tag="prep")
+                for c in range(SPREAD // P):
+                    col = (s * F2 + w * SPREAD) // P + c
+                    nc.tensor.transpose(
+                        spread[:, c * P : (c + 1) * P],
+                        b2_cols[:, col : col + 1].to_broadcast([P, P]),
+                        ident_bf[:],
+                    )
+                copy = nc.vector.tensor_copy if w % 2 == 0 else nc.scalar.copy
+                copy(out=b2_all[:, w * SPREAD : (w + 1) * SPREAD], in_=spread[:])
+
+            h_grouped = style_pool.tile([P, PASSES2, B, PACK], BF16, align_bytes=64)
+            for g in range(PASSES2):
+                w1_codes, w1_scales = quantise_block(
+                    w1_raw[s][:, :, g * K_PASS : (g + 1) * K_PASS], g
+                )
+                h_acc = h_psum.tile([P, PACK, B], F32)
+                for t in range(PACK):
+                    nc.tensor.matmul_mx(
+                        out=h_acc[:, t, :],
+                        lhsT=w1_codes[:, t * P : (t + 1) * P].bitcast(FP8X4),
+                        lhsT_scale=w1_scales[:, t * P : (t + 1) * P],
+                        rhs=x_codes[:, s * B : (s + 1) * B].bitcast(FP8X4),
+                        rhs_scale=x_scales[:, s * B : (s + 1) * B],
+                        start=True,
+                        stop=True,
+                    )
+                for t in range(PACK):
+                    row = s * (F1 // P) + g * PACK + t
+                    nc.scalar.activation(
+                        out=h_grouped[:, g, :, t],
+                        in_=h_acc[:, t, :],
+                        func=RELU,
+                        bias=b1_cols[:, row : row + 1],
+                        scale=1.0,
+                    )
+            h_codes = style_pool.tile([P, PASSES2 * B], U32, align_bytes=64)
+            h_scales = style_pool.tile([P, PASSES2 * B], U8, align_bytes=64)
+            nc.vector.quantize_mx(
+                out=h_codes[:].bitcast(FP8X4),
+                scales=h_scales[:],
+                in_=h_grouped[:].rearrange("p g b t -> p (g b t)"),
+            )
+
+            acc = []
+            for n in range(BLOCKS2):
+                bank = acc_psum.tile([P, N_PASS], F32, name="bank")
+                acc.append(bank)
+            for g in range(PASSES2):
+                for n in range(BLOCKS2):
+                    cols = slice(n * N_PASS, (n + 1) * N_PASS)
+                    w2_codes, w2_scales = quantise_block(w2_raw[s * PASSES2 + g][:, :, cols], n)
+                    nc.tensor.matmul_mx(
+                        out=acc[n][:],
+                        lhsT=h_codes[:, g * B : (g + 1) * B].bitcast(FP8X4),
+                        lhsT_scale=h_scales[:, g * B : (g + 1) * B],
+                        rhs=w2_codes[:].bitcast(FP8X4),
+                        rhs_scale=w2_scales[:],
+                        start=(g == 0),
+                        stop=(g == PASSES2 - 1),
+                    )
+                    if g == PASSES2 - 1:
+                        result = out_pool.tile([P, N_PASS], F32)
+                        nc.vector.tensor_tensor(
+                            out=result[:], in0=acc[n][:], in1=b2_all[:, cols], op=ADD
+                        )
+                        nc.sync.dma_start(out=out[:, s, cols], in_=result[:])
+
+            if s + 3 < S:
+                load_w1(s + 3)
+                load_w2(s + 3)

@@ -8,7 +8,6 @@ F32 = mybir.dt.float32
 U32 = mybir.dt.uint32
 U8 = mybir.dt.uint8
 FP8X4 = mybir.dt.float8_e4m3fn_x4
-RELU = mybir.ActivationFunctionType.Relu
 ADD = mybir.AluOpType.add
 
 P = 128
@@ -19,9 +18,18 @@ B, S, D, F1, F2 = 128, 4, 256, 1024, 2048
 K1 = 2 * D
 PASSES2 = F1 // K_PASS
 N_PASS = 512
-BLOCKS2 = F2 // N_PASS
-SPREAD = 1024
+SLAB_COLS = 1024
+PASSES_PER_SLAB = SLAB_COLS // N_PASS
+QUARTERS = F2 // SLAB_COLS
+SLABS_PER_STYLE = 1 + PASSES2 * QUARTERS
+SLABS = S * SLABS_PER_STYLE
+RESIDENT = 15
 RUN = 4
+
+VECTOR_COLS = 416
+
+SPREAD_B2_AT = 3
+COPY_B2_AT = 1
 
 FLOPS = 2 * B * S * (K1 * F1 + F1 * F2)
 
@@ -29,31 +37,148 @@ FLOPS = 2 * B * S * (K1 * F1 + F1 * F2)
 def tile_simplefusionmodule_pa_kernel(tc, x1, x2, W1, b1, W2, b2, out):
     nc = tc.nc
     with ExitStack() as ctx:
+        ctx.enter_context(tc.manual_schedule())
         const = ctx.enter_context(tc.tile_pool(name="const", bufs=1))
-        w1_pool = ctx.enter_context(tc.tile_pool(name="w1_pool", bufs=3))
-        w2_pool = ctx.enter_context(tc.tile_pool(name="w2_pool", bufs=3 * PASSES2))
-        grouped_pool = ctx.enter_context(tc.tile_pool(name="grouped_pool", bufs=6))
-        codes_pool = ctx.enter_context(tc.tile_pool(name="codes_pool", bufs=6))
+        raw_pool = ctx.enter_context(tc.tile_pool(name="raw_pool", bufs=RESIDENT))
+        grouped_pool = ctx.enter_context(tc.tile_pool(name="grouped_pool", bufs=4))
+        codes_pool = ctx.enter_context(tc.tile_pool(name="codes_pool", bufs=4))
         style_pool = ctx.enter_context(tc.tile_pool(name="style_pool", bufs=2))
-        out_pool = ctx.enter_context(tc.tile_pool(name="out_pool", bufs=S * BLOCKS2))
+        out_pool = ctx.enter_context(tc.tile_pool(name="out_pool", bufs=S * F2 // N_PASS))
         prep_psum = ctx.enter_context(tc.psum_pool(name="prep_psum", bufs=2))
-        h_psum = ctx.enter_context(tc.psum_pool(name="h_psum", bufs=2))
-        acc_psum = ctx.enter_context(tc.psum_pool(name="acc_psum", bufs=BLOCKS2))
+        h_psum = ctx.enter_context(tc.psum_pool(name="h_psum", bufs=PASSES2))
+        acc_psum = ctx.enter_context(tc.psum_pool(name="acc_psum", bufs=F2 // N_PASS))
 
-        w1_raw = []
-        w2_raw = []
+        raw_of = {}
+        grouped_of = {}
+        codes_of = {}
+        h_acc_of = {}
+        h_codes_of = {}
+        acc_of = {}
+        spread_of = {}
+        b2_of = {}
 
-        def load_w1(s):
-            w1 = w1_pool.tile([P, PACK, F1], BF16)
-            nc.sync.dma_start(out=w1[:], in_=W1[s].rearrange("(p t) f -> p t f", t=PACK))
-            w1_raw.append(w1)
+        def load(j):
+            s, r = divmod(j, SLABS_PER_STYLE)
+            raw = raw_pool.tile([P, PACK, SLAB_COLS], BF16)
+            if r == 0:
+                rows = W1[s].rearrange("(p t) f -> p t f", t=PACK)
+            else:
+                g, w = divmod(r - 1, QUARTERS)
+                part = W2[s, g * K_PASS : (g + 1) * K_PASS, w * SLAB_COLS : (w + 1) * SLAB_COLS]
+                rows = part.rearrange("(t p) n -> p t n", p=P)
+            nc.sync.dma_start(out=raw[:], in_=rows)
+            raw_of[j] = raw
 
-        def load_w2(s):
-            for g in range(PASSES2):
-                w2 = w2_pool.tile([P, PACK, F2], BF16)
-                rows = W2[s, g * K_PASS : (g + 1) * K_PASS, :]
-                nc.sync.dma_start(out=w2[:], in_=rows.rearrange("(t p) n -> p t n", p=P))
-                w2_raw.append(w2)
+        def regroup(j):
+            grouped = grouped_pool.tile([P, SLAB_COLS, PACK], BF16, align_bytes=64)
+            dst = grouped[:].rearrange("p (c i) t -> p c t i", i=RUN)
+            src = raw_of[j][:].rearrange("p t (c i) -> p c t i", i=RUN)
+            cut = VECTOR_COLS // RUN
+            nc.vector.tensor_copy(out=dst[:, :cut], in_=src[:, :cut])
+            nc.scalar.copy(out=dst[:, cut:], in_=src[:, cut:])
+            grouped_of[j] = grouped
+
+        def quantise(j):
+            codes = codes_pool.tile([P, SLAB_COLS], U32, align_bytes=64)
+            scales = codes_pool.tile([P, SLAB_COLS], U8, align_bytes=64)
+            nc.vector.quantize_mx(
+                out=codes[:].bitcast(FP8X4),
+                scales=scales[:],
+                in_=grouped_of[j][:].rearrange("p c t -> p (c t)"),
+            )
+            codes_of[j] = (codes, scales)
+
+        def multiply(j):
+            s, r = divmod(j, SLABS_PER_STYLE)
+            codes, scales = codes_of[j]
+            if r == 0:
+                h_acc_of[s] = []
+                for g in range(PASSES2):
+                    h_acc = h_psum.tile([P, PACK, B], F32)
+                    for t in range(PACK):
+                        feats = slice((g * PACK + t) * P, (g * PACK + t + 1) * P)
+                        nc.tensor.matmul_mx(
+                            out=h_acc[:, t, :],
+                            lhsT=codes[:, feats].bitcast(FP8X4),
+                            lhsT_scale=scales[:, feats],
+                            rhs=x_codes[:, s * B : (s + 1) * B].bitcast(FP8X4),
+                            rhs_scale=x_scales[:, s * B : (s + 1) * B],
+                            start=True,
+                            stop=True,
+                        )
+                    h_acc_of[s].append(h_acc)
+            else:
+                g, w = divmod(r - 1, QUARTERS)
+                h_codes, h_scales = h_codes_of[s]
+                for i in range(PASSES_PER_SLAB):
+                    n = w * PASSES_PER_SLAB + i
+                    if g == 0:
+                        bank = acc_psum.tile([P, N_PASS], F32)
+                        acc_of[(s, n)] = bank
+                    nc.tensor.matmul_mx(
+                        out=acc_of[(s, n)][:],
+                        lhsT=h_codes[:, g * B : (g + 1) * B].bitcast(FP8X4),
+                        lhsT_scale=h_scales[:, g * B : (g + 1) * B],
+                        rhs=codes[:, i * N_PASS : (i + 1) * N_PASS].bitcast(FP8X4),
+                        rhs_scale=scales[:, i * N_PASS : (i + 1) * N_PASS],
+                        start=(g == 0),
+                        stop=(g == PASSES2 - 1),
+                    )
+
+        def drain(j):
+            s, r = divmod(j, SLABS_PER_STYLE)
+            if r == 0:
+                h_grouped = style_pool.tile([P, PASSES2, B, PACK], BF16, align_bytes=64)
+                h_codes = style_pool.tile([P, PASSES2 * B], U32, align_bytes=64)
+                h_scales = style_pool.tile([P, PASSES2 * B], U8, align_bytes=64)
+                for g in range(PASSES2):
+                    first = s * (F1 // P) + g * PACK
+                    nc.vector.tensor_tensor(
+                        out=h_grouped[:, g],
+                        in0=h_acc_of[s][g][:].rearrange("p t b -> p b t"),
+                        in1=b1_cols[:, first : first + PACK].unsqueeze(1).to_broadcast([P, B, PACK]),
+                        op=ADD,
+                    )
+                for g in range(PASSES2):
+                    nc.vector.tensor_scalar_max(h_grouped[:, g], h_grouped[:, g], 0.0)
+                for g in range(PASSES2):
+                    nc.vector.quantize_mx(
+                        out=h_codes[:, g * B : (g + 1) * B].bitcast(FP8X4),
+                        scales=h_scales[:, g * B : (g + 1) * B],
+                        in_=h_grouped[:, g].rearrange("p b t -> p (b t)"),
+                    )
+                h_codes_of[s] = (h_codes, h_scales)
+            elif (r - 1) // QUARTERS == PASSES2 - 1:
+                w = (r - 1) % QUARTERS
+                for i in range(PASSES_PER_SLAB):
+                    n = w * PASSES_PER_SLAB + i
+                    cols = slice(n * N_PASS, (n + 1) * N_PASS)
+                    result = out_pool.tile([P, N_PASS], F32)
+                    nc.vector.tensor_tensor(
+                        out=result[:], in0=acc_of[(s, n)][:], in1=b2_of[s][:, cols], op=ADD
+                    )
+                    nc.sync.dma_start(out=out[:, s, cols], in_=result[:])
+
+        def spread_b2(s):
+            spread_of[s] = []
+            for w in range(QUARTERS):
+                spread = prep_psum.tile([P, SLAB_COLS], BF16, tag="prep")
+                for c in range(SLAB_COLS // P):
+                    col = (s * F2 + w * SLAB_COLS) // P + c
+                    nc.tensor.transpose(
+                        spread[:, c * P : (c + 1) * P],
+                        b2_cols[:, col : col + 1].to_broadcast([P, P]),
+                        ident_bf[:],
+                    )
+                spread_of[s].append(spread)
+
+        def copy_b2(s):
+            b2_all = style_pool.tile([P, F2], BF16)
+            for w in range(QUARTERS):
+                nc.scalar.copy(
+                    out=b2_all[:, w * SLAB_COLS : (w + 1) * SLAB_COLS], in_=spread_of[s][w][:]
+                )
+            b2_of[s] = b2_all
 
         B1_ROWS = S * F1 // P
         B2_ROWS = S * F2 // P
@@ -66,15 +191,11 @@ def tile_simplefusionmodule_pa_kernel(tc, x1, x2, W1, b1, W2, b2, out):
             in_=b2.rearrange("s (c p) -> (s c) p", p=P),
         )
         nc.vector.memset(bias_rows[B1_ROWS + B2_ROWS : P, :], 0.0)
-
         x_cat = const.tile([P, S, K1], BF16)
-        load_w1(0)
         nc.sync.dma_start(out=x_cat[:, :, 0:D], in_=x1)
         nc.sync.dma_start(out=x_cat[:, :, D:K1], in_=x2)
-        load_w2(0)
-        for s in range(1, 3):
-            load_w1(s)
-            load_w2(s)
+        for j in range(RESIDENT):
+            load(j)
 
         ident_bf = const.tile([P, P], BF16)
         make_identity(nc, ident_bf[:])
@@ -87,6 +208,8 @@ def tile_simplefusionmodule_pa_kernel(tc, x1, x2, W1, b1, W2, b2, out):
         nc.vector.tensor_copy(out=b1_cols[:], in_=bias_cols[:, 0:B1_ROWS])
         b2_cols = const.tile([P, B2_ROWS], BF16)
         nc.vector.tensor_copy(out=b2_cols[:], in_=bias_cols[:, B1_ROWS : B1_ROWS + B2_ROWS])
+
+        regroup(0)
 
         x_words = x_cat[:].bitcast(F32)
         x_grouped = const.tile([P, S, B, 2], F32, align_bytes=64)
@@ -108,94 +231,21 @@ def tile_simplefusionmodule_pa_kernel(tc, x1, x2, W1, b1, W2, b2, out):
             scales=x_scales[:],
             in_=x_grouped[:].bitcast(BF16).rearrange("p s b t -> p (s b t)"),
         )
+        spread_b2(0)
 
-        def quantise_block(raw, block):
-            grouped = grouped_pool.tile([P, N_PASS, PACK], BF16, align_bytes=64)
-            copy = nc.vector.tensor_copy if block % 2 == 0 else nc.scalar.copy
-            copy(
-                out=grouped[:].rearrange("p (c i) t -> p c t i", i=RUN),
-                in_=raw.rearrange("p t (c i) -> p c t i", i=RUN),
-            )
-            codes = codes_pool.tile([P, N_PASS], U32, align_bytes=64)
-            scales = codes_pool.tile([P, N_PASS], U8, align_bytes=64)
-            nc.vector.quantize_mx(
-                out=codes[:].bitcast(FP8X4),
-                scales=scales[:],
-                in_=grouped[:].rearrange("p c t -> p (c t)"),
-            )
-            return codes, scales
-
-        for s in range(S):
-            b2_all = style_pool.tile([P, F2], BF16)
-            for w in range(F2 // SPREAD):
-                spread = prep_psum.tile([P, SPREAD], BF16, tag="prep")
-                for c in range(SPREAD // P):
-                    col = (s * F2 + w * SPREAD) // P + c
-                    nc.tensor.transpose(
-                        spread[:, c * P : (c + 1) * P],
-                        b2_cols[:, col : col + 1].to_broadcast([P, P]),
-                        ident_bf[:],
-                    )
-                copy = nc.vector.tensor_copy if w % 2 == 0 else nc.scalar.copy
-                copy(out=b2_all[:, w * SPREAD : (w + 1) * SPREAD], in_=spread[:])
-
-            h_grouped = style_pool.tile([P, PASSES2, B, PACK], BF16, align_bytes=64)
-            for g in range(PASSES2):
-                w1_codes, w1_scales = quantise_block(
-                    w1_raw[s][:, :, g * K_PASS : (g + 1) * K_PASS], g
-                )
-                h_acc = h_psum.tile([P, PACK, B], F32)
-                for t in range(PACK):
-                    nc.tensor.matmul_mx(
-                        out=h_acc[:, t, :],
-                        lhsT=w1_codes[:, t * P : (t + 1) * P].bitcast(FP8X4),
-                        lhsT_scale=w1_scales[:, t * P : (t + 1) * P],
-                        rhs=x_codes[:, s * B : (s + 1) * B].bitcast(FP8X4),
-                        rhs_scale=x_scales[:, s * B : (s + 1) * B],
-                        start=True,
-                        stop=True,
-                    )
-                for t in range(PACK):
-                    row = s * (F1 // P) + g * PACK + t
-                    nc.scalar.activation(
-                        out=h_grouped[:, g, :, t],
-                        in_=h_acc[:, t, :],
-                        func=RELU,
-                        bias=b1_cols[:, row : row + 1],
-                        scale=1.0,
-                    )
-            h_codes = style_pool.tile([P, PASSES2 * B], U32, align_bytes=64)
-            h_scales = style_pool.tile([P, PASSES2 * B], U8, align_bytes=64)
-            nc.vector.quantize_mx(
-                out=h_codes[:].bitcast(FP8X4),
-                scales=h_scales[:],
-                in_=h_grouped[:].rearrange("p g b t -> p (g b t)"),
-            )
-
-            acc = []
-            for n in range(BLOCKS2):
-                bank = acc_psum.tile([P, N_PASS], F32, name="bank")
-                acc.append(bank)
-            for g in range(PASSES2):
-                for n in range(BLOCKS2):
-                    cols = slice(n * N_PASS, (n + 1) * N_PASS)
-                    w2_codes, w2_scales = quantise_block(w2_raw[s * PASSES2 + g][:, :, cols], n)
-                    nc.tensor.matmul_mx(
-                        out=acc[n][:],
-                        lhsT=h_codes[:, g * B : (g + 1) * B].bitcast(FP8X4),
-                        lhsT_scale=h_scales[:, g * B : (g + 1) * B],
-                        rhs=w2_codes[:].bitcast(FP8X4),
-                        rhs_scale=w2_scales[:],
-                        start=(g == 0),
-                        stop=(g == PASSES2 - 1),
-                    )
-                    if g == PASSES2 - 1:
-                        result = out_pool.tile([P, N_PASS], F32)
-                        nc.vector.tensor_tensor(
-                            out=result[:], in0=acc[n][:], in1=b2_all[:, cols], op=ADD
-                        )
-                        nc.sync.dma_start(out=out[:, s, cols], in_=result[:])
-
-            if s + 3 < S:
-                load_w1(s + 3)
-                load_w2(s + 3)
+        for step in range(1, SLABS + 3):
+            if step < SLABS:
+                regroup(step)
+                s, r = divmod(step, SLABS_PER_STYLE)
+                if r == COPY_B2_AT:
+                    copy_b2(s)
+                if r == SPREAD_B2_AT and s + 1 < S:
+                    spread_b2(s + 1)
+            if step - 1 + RESIDENT < SLABS:
+                load(step - 1 + RESIDENT)
+            if step - 1 < SLABS:
+                quantise(step - 1)
+            if 0 <= step - 3:
+                drain(step - 3)
+            if 0 <= step - 2 < SLABS:
+                multiply(step - 2)

@@ -26,7 +26,7 @@ SLABS = S * SLABS_PER_STYLE
 RESIDENT = 15
 RUN = 4
 
-VECTOR_COLS = 416
+VECTOR_COLS = 400
 
 SPREAD_B2_AT = 3
 COPY_B2_AT = 1
@@ -209,8 +209,6 @@ def tile_simplefusionmodule_pa_kernel(tc, x1, x2, W1, b1, W2, b2, out):
         b2_cols = const.tile([P, B2_ROWS], BF16)
         nc.vector.tensor_copy(out=b2_cols[:], in_=bias_cols[:, B1_ROWS : B1_ROWS + B2_ROWS])
 
-        regroup(0)
-
         x_words = x_cat[:].bitcast(F32)
         x_grouped = const.tile([P, S, B, 2], F32, align_bytes=64)
         for pair in range(S // 2):
@@ -233,7 +231,7 @@ def tile_simplefusionmodule_pa_kernel(tc, x1, x2, W1, b1, W2, b2, out):
         )
         spread_b2(0)
 
-        for step in range(1, SLABS + 3):
+        for step in range(SLABS + 3):
             if step < SLABS:
                 regroup(step)
                 s, r = divmod(step, SLABS_PER_STYLE)
@@ -241,9 +239,9 @@ def tile_simplefusionmodule_pa_kernel(tc, x1, x2, W1, b1, W2, b2, out):
                     copy_b2(s)
                 if r == SPREAD_B2_AT and s + 1 < S:
                     spread_b2(s + 1)
-            if step - 1 + RESIDENT < SLABS:
-                load(step - 1 + RESIDENT)
-            if step - 1 < SLABS:
+                if step + RESIDENT < SLABS:
+                    load(step + RESIDENT)
+            if 0 <= step - 1 < SLABS:
                 quantise(step - 1)
             if 0 <= step - 3:
                 drain(step - 3)

@@ -15,23 +15,21 @@ PACK = 4
 K_PASS = P * PACK
 
 B, S, D, F1, F2 = 128, 4, 256, 1024, 2048
-K1 = 2 * D
+STREAMS = 2
+PAIR = 2
 PASSES2 = F1 // K_PASS
 N_PASS = 512
 SLAB_COLS = 1024
 PASSES_PER_SLAB = SLAB_COLS // N_PASS
-QUARTERS = F2 // SLAB_COLS
-SLABS_PER_STYLE = 1 + PASSES2 * QUARTERS
-SLABS = S * SLABS_PER_STYLE
-RESIDENT = 15
+HALVES = F2 // SLAB_COLS
+SLABS_PER_W2 = PASSES2 * HALVES
+SLABS = S + S * SLABS_PER_W2
+RESIDENT = 14
 RUN = 4
 
 VECTOR_COLS = 400
 
-SPREAD_B2_AT = 3
-COPY_B2_AT = 1
-
-FLOPS = 2 * B * S * (K1 * F1 + F1 * F2)
+FLOPS = 2 * B * S * (STREAMS * D * F1 + F1 * F2)
 
 
 def tile_simplefusionmodule_pa_kernel(tc, x1, x2, W1, b1, W2, b2, out):
@@ -43,6 +41,7 @@ def tile_simplefusionmodule_pa_kernel(tc, x1, x2, W1, b1, W2, b2, out):
         grouped_pool = ctx.enter_context(tc.tile_pool(name="grouped_pool", bufs=4))
         codes_pool = ctx.enter_context(tc.tile_pool(name="codes_pool", bufs=4))
         style_pool = ctx.enter_context(tc.tile_pool(name="style_pool", bufs=2))
+        h_pool = ctx.enter_context(tc.tile_pool(name="h_pool", bufs=S))
         out_pool = ctx.enter_context(tc.tile_pool(name="out_pool", bufs=S * F2 // N_PASS))
         prep_psum = ctx.enter_context(tc.psum_pool(name="prep_psum", bufs=2))
         h_psum = ctx.enter_context(tc.psum_pool(name="h_psum", bufs=PASSES2))
@@ -57,16 +56,22 @@ def tile_simplefusionmodule_pa_kernel(tc, x1, x2, W1, b1, W2, b2, out):
         spread_of = {}
         b2_of = {}
 
+        def w2_place(j):
+            s, quarter = divmod(j - S, SLABS_PER_W2)
+            g, w = divmod(quarter, HALVES)
+            return s, g, w
+
         def load(j):
-            s, r = divmod(j, SLABS_PER_STYLE)
             raw = raw_pool.tile([P, PACK, SLAB_COLS], BF16)
-            if r == 0:
-                rows = W1[s].rearrange("(p t) f -> p t f", t=PACK)
+            if j < S:
+                nc.sync.dma_start(
+                    out=raw[:].rearrange("p (u e) f -> p u e f", e=PAIR),
+                    in_=W1[j].rearrange("(u p e) f -> p u e f", u=STREAMS, e=PAIR),
+                )
             else:
-                g, w = divmod(r - 1, QUARTERS)
+                s, g, w = w2_place(j)
                 part = W2[s, g * K_PASS : (g + 1) * K_PASS, w * SLAB_COLS : (w + 1) * SLAB_COLS]
-                rows = part.rearrange("(t p) n -> p t n", p=P)
-            nc.sync.dma_start(out=raw[:], in_=rows)
+                nc.sync.dma_start(out=raw[:], in_=part.rearrange("(t p) n -> p t n", p=P))
             raw_of[j] = raw
 
         def regroup(j):
@@ -89,10 +94,9 @@ def tile_simplefusionmodule_pa_kernel(tc, x1, x2, W1, b1, W2, b2, out):
             codes_of[j] = (codes, scales)
 
         def multiply(j):
-            s, r = divmod(j, SLABS_PER_STYLE)
             codes, scales = codes_of[j]
-            if r == 0:
-                h_acc_of[s] = []
+            if j < S:
+                h_acc_of[j] = []
                 for g in range(PASSES2):
                     h_acc = h_psum.tile([P, PACK, B], F32)
                     for t in range(PACK):
@@ -101,14 +105,14 @@ def tile_simplefusionmodule_pa_kernel(tc, x1, x2, W1, b1, W2, b2, out):
                             out=h_acc[:, t, :],
                             lhsT=codes[:, feats].bitcast(FP8X4),
                             lhsT_scale=scales[:, feats],
-                            rhs=x_codes[:, s * B : (s + 1) * B].bitcast(FP8X4),
-                            rhs_scale=x_scales[:, s * B : (s + 1) * B],
+                            rhs=x_codes[:, j * B : (j + 1) * B].bitcast(FP8X4),
+                            rhs_scale=x_scales[:, j * B : (j + 1) * B],
                             start=True,
                             stop=True,
                         )
-                    h_acc_of[s].append(h_acc)
+                    h_acc_of[j].append(h_acc)
             else:
-                g, w = divmod(r - 1, QUARTERS)
+                s, g, w = w2_place(j)
                 h_codes, h_scales = h_codes_of[s]
                 for i in range(PASSES_PER_SLAB):
                     n = w * PASSES_PER_SLAB + i
@@ -125,43 +129,49 @@ def tile_simplefusionmodule_pa_kernel(tc, x1, x2, W1, b1, W2, b2, out):
                         stop=(g == PASSES2 - 1),
                     )
 
+        def drain_h(s):
+            h_grouped = style_pool.tile([P, PASSES2, B, PACK], BF16, align_bytes=64)
+            h_codes = h_pool.tile([P, PASSES2 * B], U32, align_bytes=64)
+            h_scales = h_pool.tile([P, PASSES2 * B], U8, align_bytes=64)
+            for g in range(PASSES2):
+                b1_col = s * (F1 // P) + g * PACK
+                nc.vector.tensor_tensor(
+                    out=h_grouped[:, g],
+                    in0=h_acc_of[s][g][:].rearrange("p t b -> p b t"),
+                    in1=b1_cols[:, b1_col : b1_col + PACK].unsqueeze(1).to_broadcast([P, B, PACK]),
+                    op=ADD,
+                )
+            for g in range(PASSES2):
+                nc.vector.tensor_scalar_max(h_grouped[:, g], h_grouped[:, g], 0.0)
+            for g in range(PASSES2):
+                nc.vector.quantize_mx(
+                    out=h_codes[:, g * B : (g + 1) * B].bitcast(FP8X4),
+                    scales=h_scales[:, g * B : (g + 1) * B],
+                    in_=h_grouped[:, g].rearrange("p b t -> p (b t)"),
+                )
+            h_codes_of[s] = (h_codes, h_scales)
+
+        def drain_out(s, w):
+            for i in range(PASSES_PER_SLAB):
+                n = w * PASSES_PER_SLAB + i
+                cols = slice(n * N_PASS, (n + 1) * N_PASS)
+                result = out_pool.tile([P, N_PASS], F32)
+                nc.vector.tensor_tensor(
+                    out=result[:], in0=acc_of[(s, n)][:], in1=b2_of[s][:, cols], op=ADD
+                )
+                nc.sync.dma_start(out=out[:, s, cols], in_=result[:])
+
         def drain(j):
-            s, r = divmod(j, SLABS_PER_STYLE)
-            if r == 0:
-                h_grouped = style_pool.tile([P, PASSES2, B, PACK], BF16, align_bytes=64)
-                h_codes = style_pool.tile([P, PASSES2 * B], U32, align_bytes=64)
-                h_scales = style_pool.tile([P, PASSES2 * B], U8, align_bytes=64)
-                for g in range(PASSES2):
-                    first = s * (F1 // P) + g * PACK
-                    nc.vector.tensor_tensor(
-                        out=h_grouped[:, g],
-                        in0=h_acc_of[s][g][:].rearrange("p t b -> p b t"),
-                        in1=b1_cols[:, first : first + PACK].unsqueeze(1).to_broadcast([P, B, PACK]),
-                        op=ADD,
-                    )
-                for g in range(PASSES2):
-                    nc.vector.tensor_scalar_max(h_grouped[:, g], h_grouped[:, g], 0.0)
-                for g in range(PASSES2):
-                    nc.vector.quantize_mx(
-                        out=h_codes[:, g * B : (g + 1) * B].bitcast(FP8X4),
-                        scales=h_scales[:, g * B : (g + 1) * B],
-                        in_=h_grouped[:, g].rearrange("p b t -> p (b t)"),
-                    )
-                h_codes_of[s] = (h_codes, h_scales)
-            elif (r - 1) // QUARTERS == PASSES2 - 1:
-                w = (r - 1) % QUARTERS
-                for i in range(PASSES_PER_SLAB):
-                    n = w * PASSES_PER_SLAB + i
-                    cols = slice(n * N_PASS, (n + 1) * N_PASS)
-                    result = out_pool.tile([P, N_PASS], F32)
-                    nc.vector.tensor_tensor(
-                        out=result[:], in0=acc_of[(s, n)][:], in1=b2_of[s][:, cols], op=ADD
-                    )
-                    nc.sync.dma_start(out=out[:, s, cols], in_=result[:])
+            if j < S:
+                drain_h(j)
+            else:
+                s, g, w = w2_place(j)
+                if g == PASSES2 - 1:
+                    drain_out(s, w)
 
         def spread_b2(s):
             spread_of[s] = []
-            for w in range(QUARTERS):
+            for w in range(HALVES):
                 spread = prep_psum.tile([P, SLAB_COLS], BF16, tag="prep")
                 for c in range(SLAB_COLS // P):
                     col = (s * F2 + w * SLAB_COLS) // P + c
@@ -174,7 +184,7 @@ def tile_simplefusionmodule_pa_kernel(tc, x1, x2, W1, b1, W2, b2, out):
 
         def copy_b2(s):
             b2_all = style_pool.tile([P, F2], BF16)
-            for w in range(QUARTERS):
+            for w in range(HALVES):
                 nc.scalar.copy(
                     out=b2_all[:, w * SLAB_COLS : (w + 1) * SLAB_COLS], in_=spread_of[s][w][:]
                 )
@@ -191,9 +201,9 @@ def tile_simplefusionmodule_pa_kernel(tc, x1, x2, W1, b1, W2, b2, out):
             in_=b2.rearrange("s (c p) -> (s c) p", p=P),
         )
         nc.vector.memset(bias_rows[B1_ROWS + B2_ROWS : P, :], 0.0)
-        x_cat = const.tile([P, S, K1], BF16)
-        nc.sync.dma_start(out=x_cat[:, :, 0:D], in_=x1)
-        nc.sync.dma_start(out=x_cat[:, :, D:K1], in_=x2)
+        x_both = const.tile([P, STREAMS, S, D], BF16)
+        nc.sync.dma_start(out=x_both[:, 0], in_=x1)
+        nc.sync.dma_start(out=x_both[:, 1], in_=x2)
         for j in range(RESIDENT):
             load(j)
 
@@ -209,17 +219,16 @@ def tile_simplefusionmodule_pa_kernel(tc, x1, x2, W1, b1, W2, b2, out):
         b2_cols = const.tile([P, B2_ROWS], BF16)
         nc.vector.tensor_copy(out=b2_cols[:], in_=bias_cols[:, B1_ROWS : B1_ROWS + B2_ROWS])
 
-        x_words = x_cat[:].bitcast(F32)
-        x_grouped = const.tile([P, S, B, 2], F32, align_bytes=64)
-        for pair in range(S // 2):
-            x_t = prep_psum.tile([P, 2, 2, B], F32, tag="prep")
-            for i in range(2):
-                for u in range(2):
-                    nc.tensor.transpose(
-                        x_t[:, i, u, :], x_words[:, 2 * pair + i, u : K1 // 2 : 2], ident_f32[:]
-                    )
+        x_words = x_both[:].bitcast(F32)
+        x_grouped = const.tile([P, S, B, STREAMS], F32, align_bytes=64)
+        STYLES_PER_BANK = 2
+        for s0 in range(0, S, STYLES_PER_BANK):
+            x_t = prep_psum.tile([P, STYLES_PER_BANK, STREAMS, B], F32, tag="prep")
+            for i in range(STYLES_PER_BANK):
+                for u in range(STREAMS):
+                    nc.tensor.transpose(x_t[:, i, u, :], x_words[:, u, s0 + i, :], ident_f32[:])
             nc.vector.tensor_copy(
-                out=x_grouped[:, 2 * pair : 2 * pair + 2],
+                out=x_grouped[:, s0 : s0 + STYLES_PER_BANK],
                 in_=x_t[:].rearrange("p s u b -> p s b u"),
             )
         x_codes = const.tile([P, S * B], U32, align_bytes=64)
@@ -234,13 +243,14 @@ def tile_simplefusionmodule_pa_kernel(tc, x1, x2, W1, b1, W2, b2, out):
         for step in range(SLABS + 3):
             if step < SLABS:
                 regroup(step)
-                s, r = divmod(step, SLABS_PER_STYLE)
-                if r == COPY_B2_AT:
-                    copy_b2(s)
-                if r == SPREAD_B2_AT and s + 1 < S:
-                    spread_b2(s + 1)
                 if step + RESIDENT < SLABS:
                     load(step + RESIDENT)
+                if step >= S:
+                    s, g, w = w2_place(step)
+                    if (g, w) == (0, 0):
+                        copy_b2(s)
+                    if (g, w) == (0, 1) and s + 1 < S:
+                        spread_b2(s + 1)
             if 0 <= step - 1 < SLABS:
                 quantise(step - 1)
             if 0 <= step - 3:

from contextlib import ExitStack

import concourse.mybir as mybir
from concourse.masks import make_identity

BF16 = mybir.dt.bfloat16
F32 = mybir.dt.float32
U32 = mybir.dt.uint32
U8 = mybir.dt.uint8
FP8X4 = mybir.dt.float8_e4m3fn_x4
ADD = mybir.AluOpType.add

P = 128
PACK = 4
K_PASS = P * PACK

B, S, D, F1, F2 = 128, 4, 256, 1024, 2048
STREAMS = 2
PAIR = 2
PASSES2 = F1 // K_PASS
N_PASS = 512
SLAB_COLS = 1024
PASSES_PER_SLAB = SLAB_COLS // N_PASS
HALVES = F2 // SLAB_COLS
SLABS_PER_W2 = PASSES2 * HALVES
SLABS = S + S * SLABS_PER_W2
RESIDENT = 14
RUN = 4

VECTOR_COLS = 400

FLOPS = 2 * B * S * (STREAMS * D * F1 + F1 * F2)


def tile_simplefusionmodule_pa_kernel(tc, x1, x2, W1, b1, W2, b2, out):
    nc = tc.nc
    with ExitStack() as ctx:
        ctx.enter_context(tc.manual_schedule())
        const = ctx.enter_context(tc.tile_pool(name="const", bufs=1))
        raw_pool = ctx.enter_context(tc.tile_pool(name="raw_pool", bufs=RESIDENT))
        grouped_pool = ctx.enter_context(tc.tile_pool(name="grouped_pool", bufs=4))
        codes_pool = ctx.enter_context(tc.tile_pool(name="codes_pool", bufs=4))
        style_pool = ctx.enter_context(tc.tile_pool(name="style_pool", bufs=2))
        h_pool = ctx.enter_context(tc.tile_pool(name="h_pool", bufs=S))
        out_pool = ctx.enter_context(tc.tile_pool(name="out_pool", bufs=S * F2 // N_PASS))
        prep_psum = ctx.enter_context(tc.psum_pool(name="prep_psum", bufs=2))
        h_psum = ctx.enter_context(tc.psum_pool(name="h_psum", bufs=PASSES2))
        acc_psum = ctx.enter_context(tc.psum_pool(name="acc_psum", bufs=F2 // N_PASS))

        raw_of = {}
        grouped_of = {}
        codes_of = {}
        h_acc_of = {}
        h_codes_of = {}
        acc_of = {}
        spread_of = {}
        b2_of = {}

        def w2_place(j):
            s, quarter = divmod(j - S, SLABS_PER_W2)
            g, w = divmod(quarter, HALVES)
            return s, g, w

        def load(j):
            raw = raw_pool.tile([P, PACK, SLAB_COLS], BF16)
            if j < S:
                nc.sync.dma_start(
                    out=raw[:].rearrange("p (u e) f -> p u e f", e=PAIR),
                    in_=W1[j].rearrange("(u p e) f -> p u e f", u=STREAMS, e=PAIR),
                )
            else:
                s, g, w = w2_place(j)
                part = W2[s, g * K_PASS : (g + 1) * K_PASS, w * SLAB_COLS : (w + 1) * SLAB_COLS]
                nc.sync.dma_start(out=raw[:], in_=part.rearrange("(t p) n -> p t n", p=P))
            raw_of[j] = raw

        def regroup(j):
            grouped = grouped_pool.tile([P, SLAB_COLS, PACK], BF16, align_bytes=64)
            dst = grouped[:].rearrange("p (c i) t -> p c t i", i=RUN)
            src = raw_of[j][:].rearrange("p t (c i) -> p c t i", i=RUN)
            cut = VECTOR_COLS // RUN
            nc.vector.tensor_copy(out=dst[:, :cut], in_=src[:, :cut])
            nc.scalar.copy(out=dst[:, cut:], in_=src[:, cut:])
            grouped_of[j] = grouped

        def quantise(j):
            codes = codes_pool.tile([P, SLAB_COLS], U32, align_bytes=64)
            scales = codes_pool.tile([P, SLAB_COLS], U8, align_bytes=64)
            nc.vector.quantize_mx(
                out=codes[:].bitcast(FP8X4),
                scales=scales[:],
                in_=grouped_of[j][:].rearrange("p c t -> p (c t)"),
            )
            codes_of[j] = (codes, scales)

        def multiply(j):
            codes, scales = codes_of[j]
            if j < S:
                h_acc_of[j] = []
                for g in range(PASSES2):
                    h_acc = h_psum.tile([P, PACK, B], F32)
                    for t in range(PACK):
                        feats = slice((g * PACK + t) * P, (g * PACK + t + 1) * P)
                        nc.tensor.matmul_mx(
                            out=h_acc[:, t, :],
                            lhsT=codes[:, feats].bitcast(FP8X4),
                            lhsT_scale=scales[:, feats],
                            rhs=x_codes[:, j * B : (j + 1) * B].bitcast(FP8X4),
                            rhs_scale=x_scales[:, j * B : (j + 1) * B],
                            start=True,
                            stop=True,
                        )
                    h_acc_of[j].append(h_acc)
            else:
                s, g, w = w2_place(j)
                h_codes, h_scales = h_codes_of[s]
                for i in range(PASSES_PER_SLAB):
                    n = w * PASSES_PER_SLAB + i
                    if g == 0:
                        bank = acc_psum.tile([P, N_PASS], F32)
                        acc_of[(s, n)] = bank
                    nc.tensor.matmul_mx(
                        out=acc_of[(s, n)][:],
                        lhsT=h_codes[:, g * B : (g + 1) * B].bitcast(FP8X4),
                        lhsT_scale=h_scales[:, g * B : (g + 1) * B],
                        rhs=codes[:, i * N_PASS : (i + 1) * N_PASS].bitcast(FP8X4),
                        rhs_scale=scales[:, i * N_PASS : (i + 1) * N_PASS],
                        start=(g == 0),
                        stop=(g == PASSES2 - 1),
                    )

        def drain_h(s):
            h_grouped = style_pool.tile([P, PASSES2, B, PACK], BF16, align_bytes=64)
            h_codes = h_pool.tile([P, PASSES2 * B], U32, align_bytes=64)
            h_scales = h_pool.tile([P, PASSES2 * B], U8, align_bytes=64)
            for g in range(PASSES2):
                b1_col = s * (F1 // P) + g * PACK
                nc.vector.tensor_tensor(
                    out=h_grouped[:, g],
                    in0=h_acc_of[s][g][:].rearrange("p t b -> p b t"),
                    in1=b1_cols[:, b1_col : b1_col + PACK].unsqueeze(1).to_broadcast([P, B, PACK]),
                    op=ADD,
                )
            for g in range(PASSES2):
                nc.vector.tensor_scalar_max(h_grouped[:, g], h_grouped[:, g], 0.0)
            for g in range(PASSES2):
                nc.vector.quantize_mx(
                    out=h_codes[:, g * B : (g + 1) * B].bitcast(FP8X4),
                    scales=h_scales[:, g * B : (g + 1) * B],
                    in_=h_grouped[:, g].rearrange("p b t -> p (b t)"),
                )
            h_codes_of[s] = (h_codes, h_scales)

        def drain_out(s, w):
            for i in range(PASSES_PER_SLAB):
                n = w * PASSES_PER_SLAB + i
                cols = slice(n * N_PASS, (n + 1) * N_PASS)
                result = out_pool.tile([P, N_PASS], F32)
                nc.vector.tensor_tensor(
                    out=result[:], in0=acc_of[(s, n)][:], in1=b2_of[s][:, cols], op=ADD
                )
                nc.sync.dma_start(out=out[:, s, cols], in_=result[:])

        def drain(j):
            if j < S:
                drain_h(j)
            else:
                s, g, w = w2_place(j)
                if g == PASSES2 - 1:
                    drain_out(s, w)

        def spread_b2(s):
            spread_of[s] = []
            for w in range(HALVES):
                spread = prep_psum.tile([P, SLAB_COLS], BF16, tag="prep")
                for c in range(SLAB_COLS // P):
                    col = (s * F2 + w * SLAB_COLS) // P + c
                    nc.tensor.transpose(
                        spread[:, c * P : (c + 1) * P],
                        b2_cols[:, col : col + 1].to_broadcast([P, P]),
                        ident_bf[:],
                    )
                spread_of[s].append(spread)

        def copy_b2(s):
            b2_all = style_pool.tile([P, F2], BF16)
            for w in range(HALVES):
                nc.scalar.copy(
                    out=b2_all[:, w * SLAB_COLS : (w + 1) * SLAB_COLS], in_=spread_of[s][w][:]
                )
            b2_of[s] = b2_all

        B1_ROWS = S * F1 // P
        B2_ROWS = S * F2 // P
        bias_rows = const.tile([P, P], BF16)
        nc.sync.dma_start(
            out=bias_rows[0:B1_ROWS, :], in_=b1.rearrange("s (c p) -> (s c) p", p=P)
        )
        nc.sync.dma_start(
            out=bias_rows[B1_ROWS : B1_ROWS + B2_ROWS, :],
            in_=b2.rearrange("s (c p) -> (s c) p", p=P),
        )
        nc.vector.memset(bias_rows[B1_ROWS + B2_ROWS : P, :], 0.0)
        x_both = const.tile([P, STREAMS, S, D], BF16)
        nc.sync.dma_start(out=x_both[:, 0], in_=x1)
        nc.sync.dma_start(out=x_both[:, 1], in_=x2)
        for j in range(RESIDENT):
            load(j)

        ident_bf = const.tile([P, P], BF16)
        make_identity(nc, ident_bf[:])
        ident_f32 = const.tile([P, P], F32)
        make_identity(nc, ident_f32[:])

        bias_cols = prep_psum.tile([P, P], BF16, tag="prep")
        nc.tensor.transpose(bias_cols[:], bias_rows[:], ident_bf[:])
        b1_cols = const.tile([P, B1_ROWS], F32)
        nc.vector.tensor_copy(out=b1_cols[:], in_=bias_cols[:, 0:B1_ROWS])
        b2_cols = const.tile([P, B2_ROWS], BF16)
        nc.vector.tensor_copy(out=b2_cols[:], in_=bias_cols[:, B1_ROWS : B1_ROWS + B2_ROWS])

        x_words = x_both[:].bitcast(F32)
        x_grouped = const.tile([P, S, B, STREAMS], F32, align_bytes=64)
        STYLES_PER_BANK = 2
        for s0 in range(0, S, STYLES_PER_BANK):
            x_t = prep_psum.tile([P, STYLES_PER_BANK, STREAMS, B], F32, tag="prep")
            for i in range(STYLES_PER_BANK):
                for u in range(STREAMS):
                    nc.tensor.transpose(x_t[:, i, u, :], x_words[:, u, s0 + i, :], ident_f32[:])
            nc.vector.tensor_copy(
                out=x_grouped[:, s0 : s0 + STYLES_PER_BANK],
                in_=x_t[:].rearrange("p s u b -> p s b u"),
            )
        x_codes = const.tile([P, S * B], U32, align_bytes=64)
        x_scales = const.tile([P, S * B], U8, align_bytes=64)
        nc.vector.quantize_mx(
            out=x_codes[:].bitcast(FP8X4),
            scales=x_scales[:],
            in_=x_grouped[:].bitcast(BF16).rearrange("p s b t -> p (s b t)"),
        )
        spread_b2(0)

        for step in range(SLABS + 3):
            if step < SLABS:
                regroup(step)
                if step + RESIDENT < SLABS:
                    load(step + RESIDENT)
                if step >= S:
                    s, g, w = w2_place(step)
                    if (g, w) == (0, 0):
                        copy_b2(s)
                    if (g, w) == (0, 1) and s + 1 < S:
                        spread_b2(s + 1)
            if 0 <= step - 1 < SLABS:
                quantise(step - 1)
            if 0 <= step - 3:
                drain(step - 3)
            if 0 <= step - 2 < SLABS:
                multiply(step - 2)
